import numpy as np
import ml_dtypes


def mxq(x, axis, fmt="e4m3"):
    dtype, down = {"e4m3": (ml_dtypes.float8_e4m3fn, 7), "e5m2": (ml_dtypes.float8_e5m2, 14)}[fmt]
    v = np.moveaxis(np.asarray(x, np.float32).astype(ml_dtypes.bfloat16).astype(np.float64), axis, -1)
    blocks = v.reshape(v.shape[:-1] + (-1, 32))
    amax = np.abs(blocks).max(-1, keepdims=True)
    byte = np.maximum(np.where(amax > 0, np.frexp(amax)[1] - 1 + 127, 0) - down, 1)
    scale = np.exp2(byte - 127.0)
    codes = (blocks / scale).astype(np.float32).astype(dtype).astype(np.float64)
    return np.moveaxis((codes * scale).reshape(v.shape), -1, axis)


WIDE = False


def mx_kscale(k):
    if not WIDE:
        return np.ones(k)
    levels = np.array([10, -10, 5, -5, 0])
    a = np.random.permutation(np.resize(levels, k // 512 * 4)).reshape(k // 512, 4)
    idx = np.arange(k)
    return np.exp2(a[idx // 512, idx % 128 // 32])


BF16 = ml_dtypes.bfloat16


def bf(x):
    return np.asarray(x, np.float32).astype(BF16)


def f64(x):
    return np.asarray(x).astype(np.float64)


B, D, H, W, K = 2, 512, 128, 128, 128
N = H * W
EPS = 1e-08


def softmax(v):
    e = np.exp(v - v.max(-1, keepdims=True))
    return e / e.sum(-1, keepdims=True)


def setup_inputs():
    s = mx_kscale(D)
    return {"x": bf(np.random.standard_normal((B, D, H, W)) * s[None, :, None, None]),
            "conv_w": bf(np.random.standard_normal((K, D)) * np.sqrt(2.0 / D) / s[None, :]),
            "centroids": bf(np.random.standard_normal((K, D)) * np.sqrt(2.0 / D) * s[None, :])}


def reference(x, conv_w, centroids):
    d = f64(x).reshape(B, D, N).transpose(0, 2, 1)
    logits = (mxq(d, 2, "e4m3") @ mxq(f64(conv_w), 1, "e4m3").T) + EPS
    w = softmax(logits)
    vlad = (mxq(w, 1, "e4m3").transpose(0, 2, 1) @ mxq(d, 1, "e4m3")) - w.sum(1)[..., None] * f64(centroids)[None]
    return vlad.reshape(B, -1)

@@ -1,0 +1,224 @@
+from contextlib import ExitStack
+
+import concourse.mybir as mybir
+from concourse.masks import make_identity
+
+F32 = mybir.dt.float32
+BF16 = mybir.dt.bfloat16
+U32 = mybir.dt.uint32
+U8 = mybir.dt.uint8
+FP8X4 = mybir.dt.float8_e4m3fn_x4
+ALU = mybir.AluOpType
+ACT = mybir.ActivationFunctionType
+AXIS = mybir.AxisListType
+
+P = 128
+PACK = 4
+IMAGES = 2
+CHANNELS = 512
+POSITIONS = 16384
+CLUSTERS = 128
+
+PASS = P * PACK
+HALF = PASS // 2
+ROUND = 2 * PASS
+CHUNK = 2 * ROUND
+PASSES_PER_ROUND = ROUND // PASS
+PAIRS = ROUND // 2
+
+VECTOR_PAIRS = 256
+
+FLOPS = 2 * 2 * IMAGES * POSITIONS * CHANNELS * CLUSTERS
+
+
+def tile_netvlad_k_kernel(tc, x, conv_w, centroids, out):
+    nc = tc.nc
+    x_rows = x.rearrange("b (q j) h w -> b q j (h w)", j=PACK)
+    out_rows = out.rearrange("b (k c) -> b k c", c=CHANNELS)
+
+    with ExitStack() as ctx:
+        const = ctx.enter_context(tc.tile_pool(name="const", bufs=1))
+        loads = ctx.enter_context(tc.tile_pool(name="loads", bufs=3))
+        work = ctx.enter_context(tc.tile_pool(name="work", bufs=3))
+        small = ctx.enter_context(tc.tile_pool(name="small", bufs=4))
+        sums = ctx.enter_context(tc.psum_pool(name="sums", bufs=1))
+        logit_banks = ctx.enter_context(tc.psum_pool(name="logit_banks", bufs=2))
+        flip_banks = ctx.enter_context(tc.psum_pool(name="flip_banks", bufs=4))
+
+        identity = const.tile([P, P], F32)
+        make_identity(nc, identity[:])
+
+        centroid_sb = const.tile([P, CHANNELS], BF16)
+        nc.scalar.dma_start(out=centroid_sb[:], in_=centroids)
+
+        conv_sb = const.tile([P, CHANNELS], BF16)
+        nc.scalar.dma_start(out=conv_sb[:], in_=conv_w)
+        conv_words = conv_sb[:].bitcast(F32).rearrange("k (q u) -> k u q", u=2)
+        conv_flip = flip_banks.tile([P, 2, 2 * P], F32, tag="flip")
+        for u in range(2):
+            nc.tensor.transpose(conv_flip[:, u, 0:P], conv_words[:, u, :], identity[:])
+        conv_grouped = const.tile([P, CLUSTERS, PACK], BF16, align_bytes=64)
+        nc.vector.tensor_copy(
+            out=conv_grouped[:].bitcast(F32),
+            in_=conv_flip[:, :, 0:P].rearrange("q u k -> q k u"),
+        )
+        conv_codes = const.tile([P, CLUSTERS], U32, align_bytes=64)
+        conv_scales = const.tile([P, CLUSTERS], U8, align_bytes=64)
+        nc.vector.quantize_mx(
+            out=conv_codes[:].bitcast(FP8X4),
+            scales=conv_scales[:],
+            in_=conv_grouped[:].rearrange("q k t -> q (k t)"),
+        )
+
+        for b in range(IMAGES):
+            vlad_acc = sums.tile([P, CHANNELS], F32)
+            wsum_acc = sums.tile([P, 1], F32)
+            for chunk in range(POSITIONS // CHUNK):
+                x_sb = loads.tile([P, PACK, CHUNK], BF16)
+                nc.sync.dma_start(
+                    out=x_sb[:], in_=x_rows[b, :, :, chunk * CHUNK : (chunk + 1) * CHUNK]
+                )
+                x_words = x_sb[:].bitcast(F32)
+
+                for r in range(CHUNK // ROUND):
+                    by_channel = work.tile([P, 2, PAIRS, PACK], BF16, align_bytes=64)
+                    src = x_sb[:, :, r * ROUND : (r + 1) * ROUND].rearrange(
+                        "q j (m e) -> q m j e", e=2
+                    )
+                    dst = by_channel[:].rearrange("q e m j -> q m j e")
+                    nc.vector.tensor_copy(
+                        out=dst[:, 0:VECTOR_PAIRS], in_=src[:, 0:VECTOR_PAIRS]
+                    )
+                    nc.scalar.copy(out=dst[:, VECTOR_PAIRS:PAIRS], in_=src[:, VECTOR_PAIRS:PAIRS])
+                    xc_codes = work.tile([P, ROUND], U32, align_bytes=64)
+                    xc_scales = work.tile([P, ROUND], U8, align_bytes=64)
+                    nc.vector.quantize_mx(
+                        out=xc_codes[:].bitcast(FP8X4),
+                        scales=xc_scales[:],
+                        in_=by_channel[:].rearrange("q e m j -> q (e m j)"),
+                    )
+
+                    by_position = work.tile(
+                        [P, PASSES_PER_ROUND, CHANNELS, PACK], BF16, align_bytes=64
+                    )
+                    w_grouped = work.tile(
+                        [P, PASSES_PER_ROUND, CLUSTERS, PACK], BF16, align_bytes=64
+                    )
+                    for g in range(PASSES_PER_ROUND):
+                        first = chunk == 0 and r == 0 and g == 0
+                        last = (
+                            chunk == POSITIONS // CHUNK - 1
+                            and r == CHUNK // ROUND - 1
+                            and g == PASSES_PER_ROUND - 1
+                        )
+                        word0 = (r * ROUND + g * PASS) // 2
+                        for jj in range(PACK // 2):
+                            flip = flip_banks.tile([P, 2, 2 * P], F32, tag="flip")
+                            for u in range(2):
+                                for j2 in range(2):
+                                    nc.tensor.transpose(
+                                        flip[:, u, j2 * P : (j2 + 1) * P],
+                                        x_words[
+                                            :, 2 * jj + j2, word0 + u * P : word0 + (u + 1) * P
+                                        ],
+                                        identity[:],
+                                    )
+                            nc.scalar.copy(
+                                out=by_position[
+                                    :, g, jj * 2 * P : (jj + 1) * 2 * P, :
+                                ].bitcast(F32),
+                                in_=flip[:].rearrange("p u c -> p c u"),
+                            )
+
+                        logits = logit_banks.tile([P, PACK, CLUSTERS], F32)
+                        for u in range(2):
+                            for e in range(2):
+                                col0 = e * PAIRS + (2 * g + u) * P
+                                nc.tensor.matmul_mx(
+                                    out=logits[:, 2 * u + e, :],
+                                    lhsT=xc_codes[:, col0 : col0 + P].bitcast(FP8X4),
+                                    lhsT_scale=xc_scales[:, col0 : col0 + P],
+                                    rhs=conv_codes[:].bitcast(FP8X4),
+                                    rhs_scale=conv_scales[:],
+                                    start=True,
+                                    stop=True,
+                                )
+
+                        neg_max = small.tile([P, PACK], F32)
+                        nc.vector.tensor_reduce(
+                            out=neg_max[:], in_=logits[:], axis=AXIS.X, op=ALU.max, negate=True
+                        )
+                        expo = work.tile([P, PACK, CLUSTERS], F32)
+                        total = small.tile([P, PACK], F32)
+                        for t in range(PACK):
+                            nc.scalar.activation(
+                                out=expo[:, t, :],
+                                in_=logits[:, t, :],
+                                func=ACT.Exp,
+                                bias=neg_max[:, t : t + 1],
+                                scale=1.0,
+                                accum_out=total[:, t : t + 1],
+                            )
+                        inv_total = small.tile([P, PACK], F32)
+                        nc.vector.reciprocal(out=inv_total[:], in_=total[:])
+                        nc.vector.tensor_tensor(
+                            out=w_grouped[:, g, :, :],
+                            in0=expo[:].rearrange("p t k -> p k t"),
+                            in1=inv_total[:].unsqueeze(1).to_broadcast([P, CLUSTERS, PACK]),
+                            op=ALU.mult,
+                        )
+                        for t in range(PACK):
+                            nc.tensor.matmul(
+                                out=wsum_acc[:],
+                                lhsT=expo[:, t, :],
+                                rhs=inv_total[:, t : t + 1],
+                                start=(first and t == 0),
+                                stop=(last and t == PACK - 1),
+                            )
+
+                    xp_codes = work.tile([P, PASSES_PER_ROUND, CHANNELS], U32, align_bytes=64)
+                    xp_scales = work.tile([P, PASSES_PER_ROUND, CHANNELS], U8, align_bytes=64)
+                    nc.vector.quantize_mx(
+                        out=xp_codes[:].rearrange("p g c -> p (g c)").bitcast(FP8X4),
+                        scales=xp_scales[:].rearrange("p g c -> p (g c)"),
+                        in_=by_position[:].rearrange("p g c t -> p (g c t)"),
+                    )
+                    w_codes = work.tile([P, PASSES_PER_ROUND, CLUSTERS], U32, align_bytes=64)
+                    w_scales = work.tile([P, PASSES_PER_ROUND, CLUSTERS], U8, align_bytes=64)
+                    nc.vector.quantize_mx(
+                        out=w_codes[:].rearrange("p g k -> p (g k)").bitcast(FP8X4),
+                        scales=w_scales[:].rearrange("p g k -> p (g k)"),
+                        in_=w_grouped[:].rearrange("p g k t -> p (g k t)"),
+                    )
+
+                    for g in range(PASSES_PER_ROUND):
+                        first = chunk == 0 and r == 0 and g == 0
+                        last = (
+                            chunk == POSITIONS // CHUNK - 1
+                            and r == CHUNK // ROUND - 1
+                            and g == PASSES_PER_ROUND - 1
+                        )
+                        nc.tensor.matmul_mx(
+                            out=vlad_acc[:],
+                            lhsT=w_codes[:, g, :].bitcast(FP8X4),
+                            lhsT_scale=w_scales[:, g, :],
+                            rhs=xp_codes[:, g, :].bitcast(FP8X4),
+                            rhs_scale=xp_scales[:, g, :],
+                            start=first,
+                            stop=last,
+                        )
+
+            neg_wsum = small.tile([P, 1], F32)
+            nc.vector.tensor_scalar(
+                out=neg_wsum[:], in0=wsum_acc[:], scalar1=-1.0, scalar2=None, op0=ALU.mult
+            )
+            result = work.tile([P, CHANNELS], F32)
+            nc.vector.scalar_tensor_tensor(
+                out=result[:],
+                in0=centroid_sb[:],
+                scalar=neg_wsum[:, 0:1],
+                in1=vlad_acc[:].rearrange("k (j q) -> k q j", j=PACK),
+                op0=ALU.mult,
+                op1=ALU.add,
+            )
+            nc.sync.dma_start(out=out_rows[b], in_=result[:])

@@ -20,11 +20,12 @@ POSITIONS = 16384
 CLUSTERS = 128
 
 PASS = P * PACK
-HALF = PASS // 2
 ROUND = 2 * PASS
-CHUNK = 2 * ROUND
-PASSES_PER_ROUND = ROUND // PASS
+PASSES = ROUND // PASS
 PAIRS = ROUND // 2
+ROUNDS_PER_IMAGE = POSITIONS // ROUND
+ROUNDS = IMAGES * ROUNDS_PER_IMAGE
+LOAD_AHEAD = 3
 
 VECTOR_PAIRS = 256
 
@@ -38,12 +39,11 @@ def tile_netvlad_k_kernel(tc, x, conv_w, centroids, out):
 
     with ExitStack() as ctx:
         const = ctx.enter_context(tc.tile_pool(name="const", bufs=1))
-        loads = ctx.enter_context(tc.tile_pool(name="loads", bufs=3))
+        loads = ctx.enter_context(tc.tile_pool(name="loads", bufs=LOAD_AHEAD + 2))
         work = ctx.enter_context(tc.tile_pool(name="work", bufs=3))
-        small = ctx.enter_context(tc.tile_pool(name="small", bufs=4))
         sums = ctx.enter_context(tc.psum_pool(name="sums", bufs=1))
-        logit_banks = ctx.enter_context(tc.psum_pool(name="logit_banks", bufs=2))
-        flip_banks = ctx.enter_context(tc.psum_pool(name="flip_banks", bufs=4))
+        logit_banks = ctx.enter_context(tc.psum_pool(name="logit_banks", bufs=PASSES))
+        flip_banks = ctx.enter_context(tc.psum_pool(name="flip_banks", bufs=2 * PASSES))
 
         identity = const.tile([P, P], F32)
         make_identity(nc, identity[:])
@@ -70,155 +70,226 @@ def tile_netvlad_k_kernel(tc, x, conv_w, centroids, out):
             in_=conv_grouped[:].rearrange("q k t -> q (k t)"),
         )
 
-        for b in range(IMAGES):
-            vlad_acc = sums.tile([P, CHANNELS], F32)
-            wsum_acc = sums.tile([P, 1], F32)
-            for chunk in range(POSITIONS // CHUNK):
-                x_sb = loads.tile([P, PACK, CHUNK], BF16)
-                nc.sync.dma_start(
-                    out=x_sb[:], in_=x_rows[b, :, :, chunk * CHUNK : (chunk + 1) * CHUNK]
-                )
-                x_words = x_sb[:].bitcast(F32)
+        x_sb = {}
+        by_channel = {}
+        xc_codes = {}
+        xc_scales = {}
+        flips = {}
+        by_position = {}
+        xp_codes = {}
+        xp_scales = {}
+        logits = {}
+        neg_max = {}
+        expo = {}
+        inv_total = {}
+        w_grouped = {}
+        w_codes = {}
+        w_scales = {}
+        vlad_acc = {}
+        wsum_acc = {}
 
-                for r in range(CHUNK // ROUND):
-                    by_channel = work.tile([P, 2, PAIRS, PACK], BF16, align_bytes=64)
-                    src = x_sb[:, :, r * ROUND : (r + 1) * ROUND].rearrange(
-                        "q j (m e) -> q m j e", e=2
-                    )
-                    dst = by_channel[:].rearrange("q e m j -> q m j e")
-                    nc.vector.tensor_copy(
-                        out=dst[:, 0:VECTOR_PAIRS], in_=src[:, 0:VECTOR_PAIRS]
-                    )
-                    nc.scalar.copy(out=dst[:, VECTOR_PAIRS:PAIRS], in_=src[:, VECTOR_PAIRS:PAIRS])
-                    xc_codes = work.tile([P, ROUND], U32, align_bytes=64)
-                    xc_scales = work.tile([P, ROUND], U8, align_bytes=64)
-                    nc.vector.quantize_mx(
-                        out=xc_codes[:].bitcast(FP8X4),
-                        scales=xc_scales[:],
-                        in_=by_channel[:].rearrange("q e m j -> q (e m j)"),
-                    )
+        def load(r):
+            b, i = divmod(r, ROUNDS_PER_IMAGE)
+            tile = loads.tile([P, PACK, ROUND], BF16, name="x_sb")
+            nc.sync.dma_start(out=tile[:], in_=x_rows[b, :, :, i * ROUND : (i + 1) * ROUND])
+            x_sb[r] = tile
 
-                    by_position = work.tile(
-                        [P, PASSES_PER_ROUND, CHANNELS, PACK], BF16, align_bytes=64
-                    )
-                    w_grouped = work.tile(
-                        [P, PASSES_PER_ROUND, CLUSTERS, PACK], BF16, align_bytes=64
-                    )
-                    for g in range(PASSES_PER_ROUND):
-                        first = chunk == 0 and r == 0 and g == 0
-                        last = (
-                            chunk == POSITIONS // CHUNK - 1
-                            and r == CHUNK // ROUND - 1
-                            and g == PASSES_PER_ROUND - 1
-                        )
-                        word0 = (r * ROUND + g * PASS) // 2
-                        for jj in range(PACK // 2):
-                            flip = flip_banks.tile([P, 2, 2 * P], F32, tag="flip")
-                            for u in range(2):
-                                for j2 in range(2):
-                                    nc.tensor.transpose(
-                                        flip[:, u, j2 * P : (j2 + 1) * P],
-                                        x_words[
-                                            :, 2 * jj + j2, word0 + u * P : word0 + (u + 1) * P
-                                        ],
-                                        identity[:],
-                                    )
-                            nc.scalar.copy(
-                                out=by_position[
-                                    :, g, jj * 2 * P : (jj + 1) * 2 * P, :
-                                ].bitcast(F32),
-                                in_=flip[:].rearrange("p u c -> p c u"),
-                            )
+        def regroup_by_channel(r):
+            tile = work.tile([P, 2, PAIRS, PACK], BF16, align_bytes=64, name="by_channel")
+            src = x_sb[r][:].rearrange("q j (m e) -> q m j e", e=2)
+            dst = tile[:].rearrange("q e m j -> q m j e")
+            nc.vector.tensor_copy(out=dst[:, 0:VECTOR_PAIRS], in_=src[:, 0:VECTOR_PAIRS])
+            nc.scalar.copy(out=dst[:, VECTOR_PAIRS:PAIRS], in_=src[:, VECTOR_PAIRS:PAIRS])
+            by_channel[r] = tile
 
-                        logits = logit_banks.tile([P, PACK, CLUSTERS], F32)
-                        for u in range(2):
-                            for e in range(2):
-                                col0 = e * PAIRS + (2 * g + u) * P
-                                nc.tensor.matmul_mx(
-                                    out=logits[:, 2 * u + e, :],
-                                    lhsT=xc_codes[:, col0 : col0 + P].bitcast(FP8X4),
-                                    lhsT_scale=xc_scales[:, col0 : col0 + P],
-                                    rhs=conv_codes[:].bitcast(FP8X4),
-                                    rhs_scale=conv_scales[:],
-                                    start=True,
-                                    stop=True,
-                                )
-
-                        neg_max = small.tile([P, PACK], F32)
-                        nc.vector.tensor_reduce(
-                            out=neg_max[:], in_=logits[:], axis=AXIS.X, op=ALU.max, negate=True
-                        )
-                        expo = work.tile([P, PACK, CLUSTERS], F32)
-                        total = small.tile([P, PACK], F32)
-                        for t in range(PACK):
-                            nc.scalar.activation(
-                                out=expo[:, t, :],
-                                in_=logits[:, t, :],
-                                func=ACT.Exp,
-                                bias=neg_max[:, t : t + 1],
-                                scale=1.0,
-                                accum_out=total[:, t : t + 1],
-                            )
-                        inv_total = small.tile([P, PACK], F32)
-                        nc.vector.reciprocal(out=inv_total[:], in_=total[:])
-                        nc.vector.tensor_tensor(
-                            out=w_grouped[:, g, :, :],
-                            in0=expo[:].rearrange("p t k -> p k t"),
-                            in1=inv_total[:].unsqueeze(1).to_broadcast([P, CLUSTERS, PACK]),
-                            op=ALU.mult,
-                        )
-                        for t in range(PACK):
-                            nc.tensor.matmul(
-                                out=wsum_acc[:],
-                                lhsT=expo[:, t, :],
-                                rhs=inv_total[:, t : t + 1],
-                                start=(first and t == 0),
-                                stop=(last and t == PACK - 1),
-                            )
-
-                    xp_codes = work.tile([P, PASSES_PER_ROUND, CHANNELS], U32, align_bytes=64)
-                    xp_scales = work.tile([P, PASSES_PER_ROUND, CHANNELS], U8, align_bytes=64)
-                    nc.vector.quantize_mx(
-                        out=xp_codes[:].rearrange("p g c -> p (g c)").bitcast(FP8X4),
-                        scales=xp_scales[:].rearrange("p g c -> p (g c)"),
-                        in_=by_position[:].rearrange("p g c t -> p (g c t)"),
-                    )
-                    w_codes = work.tile([P, PASSES_PER_ROUND, CLUSTERS], U32, align_bytes=64)
-                    w_scales = work.tile([P, PASSES_PER_ROUND, CLUSTERS], U8, align_bytes=64)
-                    nc.vector.quantize_mx(
-                        out=w_codes[:].rearrange("p g k -> p (g k)").bitcast(FP8X4),
-                        scales=w_scales[:].rearrange("p g k -> p (g k)"),
-                        in_=w_grouped[:].rearrange("p g k t -> p (g k t)"),
-                    )
-
-                    for g in range(PASSES_PER_ROUND):
-                        first = chunk == 0 and r == 0 and g == 0
-                        last = (
-                            chunk == POSITIONS // CHUNK - 1
-                            and r == CHUNK // ROUND - 1
-                            and g == PASSES_PER_ROUND - 1
-                        )
-                        nc.tensor.matmul_mx(
-                            out=vlad_acc[:],
-                            lhsT=w_codes[:, g, :].bitcast(FP8X4),
-                            lhsT_scale=w_scales[:, g, :],
-                            rhs=xp_codes[:, g, :].bitcast(FP8X4),
-                            rhs_scale=xp_scales[:, g, :],
-                            start=first,
-                            stop=last,
-                        )
-
-            neg_wsum = small.tile([P, 1], F32)
-            nc.vector.tensor_scalar(
-                out=neg_wsum[:], in0=wsum_acc[:], scalar1=-1.0, scalar2=None, op0=ALU.mult
+        def quantise_by_channel(r):
+            codes = work.tile([P, ROUND], U32, align_bytes=64, name="xc_codes")
+            scales = work.tile([P, ROUND], U8, align_bytes=64, name="xc_scales")
+            nc.vector.quantize_mx(
+                out=codes[:].bitcast(FP8X4),
+                scales=scales[:],
+                in_=by_channel[r][:].rearrange("q e m j -> q (e m j)"),
             )
-            result = work.tile([P, CHANNELS], F32)
+            xc_codes[r] = codes
+            xc_scales[r] = scales
+
+        def transpose_positions(r):
+            x_words = x_sb[r][:].bitcast(F32)
+            flips[r] = []
+            for g in range(PASSES):
+                for jj in range(PACK // 2):
+                    flip = flip_banks.tile([P, 2, 2 * P], F32, tag="flip", name="flip")
+                    for u in range(2):
+                        for j2 in range(2):
+                            word0 = (2 * g + u) * P
+                            nc.tensor.transpose(
+                                flip[:, u, j2 * P : (j2 + 1) * P],
+                                x_words[:, 2 * jj + j2, word0 : word0 + P],
+                                identity[:],
+                            )
+                    flips[r].append(flip)
+
+        def regroup_by_position(r):
+            tile = work.tile([P, PASSES, CHANNELS, PACK], BF16, align_bytes=64, name="by_position")
+            for g in range(PASSES):
+                for jj in range(PACK // 2):
+                    nc.scalar.copy(
+                        out=tile[:, g, jj * 2 * P : (jj + 1) * 2 * P, :].bitcast(F32),
+                        in_=flips[r][g * (PACK // 2) + jj][:].rearrange("p u c -> p c u"),
+                    )
+            by_position[r] = tile
+
+        def quantise_by_position(r):
+            codes = work.tile([P, PASSES, CHANNELS], U32, align_bytes=64, name="xp_codes")
+            scales = work.tile([P, PASSES, CHANNELS], U8, align_bytes=64, name="xp_scales")
+            nc.vector.quantize_mx(
+                out=codes[:].rearrange("p g c -> p (g c)").bitcast(FP8X4),
+                scales=scales[:].rearrange("p g c -> p (g c)"),
+                in_=by_position[r][:].rearrange("p g c t -> p (g c t)"),
+            )
+            xp_codes[r] = codes
+            xp_scales[r] = scales
+
+        def first_matmul(r):
+            logits[r] = []
+            for g in range(PASSES):
+                bank = logit_banks.tile([P, PACK, CLUSTERS], F32, name="logits")
+                for u in range(2):
+                    for e in range(2):
+                        col0 = e * PAIRS + (2 * g + u) * P
+                        nc.tensor.matmul_mx(
+                            out=bank[:, 2 * u + e, :],
+                            lhsT=xc_codes[r][:, col0 : col0 + P].bitcast(FP8X4),
+                            lhsT_scale=xc_scales[r][:, col0 : col0 + P],
+                            rhs=conv_codes[:].bitcast(FP8X4),
+                            rhs_scale=conv_scales[:],
+                            start=True,
+                            stop=True,
+                        )
+                logits[r].append(bank)
+
+        def row_max(r):
+            tile = work.tile([P, PASSES, PACK], F32, name="neg_max")
+            for g in range(PASSES):
+                nc.vector.tensor_reduce(
+                    out=tile[:, g, :], in_=logits[r][g][:], axis=AXIS.X, op=ALU.max, negate=True
+                )
+            neg_max[r] = tile
+
+        def exponentials(r):
+            tile = work.tile([P, PASSES, PACK, CLUSTERS], F32, name="expo")
+            total = work.tile([P, PASSES, PACK], F32, name="total")
+            for g in range(PASSES):
+                for t in range(PACK):
+                    nc.scalar.activation(
+                        out=tile[:, g, t, :],
+                        in_=logits[r][g][:, t, :],
+                        func=ACT.Exp,
+                        bias=neg_max[r][:, g, t : t + 1],
+                        scale=1.0,
+                        accum_out=total[:, g, t : t + 1],
+                    )
+            expo[r] = tile
+            inv_total[r] = total
+
+        def normalise(r):
+            inv = work.tile([P, PASSES, PACK], F32, name="inv_total")
+            nc.vector.reciprocal(out=inv[:], in_=inv_total[r][:])
+            inv_total[r] = inv
+            tile = work.tile([P, PASSES, CLUSTERS, PACK], BF16, align_bytes=64, name="w_grouped")
+            nc.vector.tensor_tensor(
+                out=tile[:],
+                in0=expo[r][:].rearrange("p g t k -> p g k t"),
+                in1=inv[:].unsqueeze(2).to_broadcast([P, PASSES, CLUSTERS, PACK]),
+                op=ALU.mult,
+            )
+            w_grouped[r] = tile
+
+        def quantise_w(r):
+            codes = work.tile([P, PASSES, CLUSTERS], U32, align_bytes=64, name="w_codes")
+            scales = work.tile([P, PASSES, CLUSTERS], U8, align_bytes=64, name="w_scales")
+            nc.vector.quantize_mx(
+                out=codes[:].rearrange("p g k -> p (g k)").bitcast(FP8X4),
+                scales=scales[:].rearrange("p g k -> p (g k)"),
+                in_=w_grouped[r][:].rearrange("p g k t -> p (g k t)"),
+            )
+            w_codes[r] = codes
+            w_scales[r] = scales
+
+        def sum_w(r):
+            b, i = divmod(r, ROUNDS_PER_IMAGE)
+            if i == 0:
+                acc = sums.tile([P, 1], F32, name="wsum_acc")
+                wsum_acc[b] = acc
+            for g in range(PASSES):
+                for t in range(PACK):
+                    nc.tensor.matmul(
+                        out=wsum_acc[b][:],
+                        lhsT=expo[r][:, g, t, :],
+                        rhs=inv_total[r][:, g, t : t + 1],
+                        start=(i == 0 and g == 0 and t == 0),
+                        stop=(i == ROUNDS_PER_IMAGE - 1 and g == PASSES - 1 and t == PACK - 1),
+                    )
+
+        def second_matmul(r):
+            b, i = divmod(r, ROUNDS_PER_IMAGE)
+            if i == 0:
+                acc = sums.tile([P, CHANNELS], F32, name="vlad_acc")
+                vlad_acc[b] = acc
+            for g in range(PASSES):
+                nc.tensor.matmul_mx(
+                    out=vlad_acc[b][:],
+                    lhsT=w_codes[r][:, g, :].bitcast(FP8X4),
+                    lhsT_scale=w_scales[r][:, g, :],
+                    rhs=xp_codes[r][:, g, :].bitcast(FP8X4),
+                    rhs_scale=xp_scales[r][:, g, :],
+                    start=(i == 0 and g == 0),
+                    stop=(i == ROUNDS_PER_IMAGE - 1 and g == PASSES - 1),
+                )
+
+        def finish_image(b):
+            neg_wsum = work.tile([P, 1], F32, name="neg_wsum")
+            nc.vector.tensor_scalar(
+                out=neg_wsum[:], in0=wsum_acc[b][:], scalar1=-1.0, scalar2=None, op0=ALU.mult
+            )
+            result = work.tile([P, CHANNELS], F32, name="result")
             nc.vector.scalar_tensor_tensor(
                 out=result[:],
                 in0=centroid_sb[:],
                 scalar=neg_wsum[:, 0:1],
-                in1=vlad_acc[:].rearrange("k (j q) -> k q j", j=PACK),
+                in1=vlad_acc[b][:].rearrange("k (j q) -> k q j", j=PACK),
                 op0=ALU.mult,
                 op1=ALU.add,
             )
             nc.sync.dma_start(out=out_rows[b], in_=result[:])
+
+        def is_round(r):
+            return 0 <= r < ROUNDS
+
+        with tc.manual_schedule():
+            for s in range(-LOAD_AHEAD, ROUNDS + 1):
+                if is_round(s + LOAD_AHEAD):
+                    load(s + LOAD_AHEAD)
+                if is_round(s + 1):
+                    transpose_positions(s + 1)
+                if is_round(s):
+                    row_max(s)
+                    exponentials(s)
+                if is_round(s + 1):
+                    quantise_by_channel(s + 1)
+                if is_round(s - 1):
+                    second_matmul(s - 1)
+                    if s % ROUNDS_PER_IMAGE == 0:
+                        finish_image(s // ROUNDS_PER_IMAGE - 1)
+                if is_round(s + 1):
+                    first_matmul(s + 1)
+                if is_round(s + 2):
+                    regroup_by_channel(s + 2)
+                if is_round(s):
+                    normalise(s)
+                    sum_w(s)
+                if is_round(s + 1):
+                    regroup_by_position(s + 1)
+                if is_round(s):
+                    quantise_by_position(s)
+                    quantise_w(s)

@@ -25,6 +25,7 @@ PASSES = ROUND // PASS
 PAIRS = ROUND // 2
 ROUNDS_PER_IMAGE = POSITIONS // ROUND
 ROUNDS = IMAGES * ROUNDS_PER_IMAGE
+SUM_COPIES = 96
 LOAD_AHEAD = 3
 
 VECTOR_PAIRS = 256
@@ -219,14 +220,14 @@ def tile_netvlad_k_kernel(tc, x, conv_w, centroids, out):
         def sum_w(r):
             b, i = divmod(r, ROUNDS_PER_IMAGE)
             if i == 0:
-                acc = sums.tile([P, 1], F32, name="wsum_acc")
+                acc = sums.tile([P, SUM_COPIES], F32, name="wsum_acc")
                 wsum_acc[b] = acc
             for g in range(PASSES):
                 for t in range(PACK):
                     nc.tensor.matmul(
                         out=wsum_acc[b][:],
                         lhsT=expo[r][:, g, t, :],
-                        rhs=inv_total[r][:, g, t : t + 1],
+                        rhs=inv_total[r][:, g, t : t + 1].to_broadcast([P, SUM_COPIES]),
                         start=(i == 0 and g == 0 and t == 0),
                         stop=(i == ROUNDS_PER_IMAGE - 1 and g == PASSES - 1 and t == PACK - 1),
                     )
@@ -250,7 +251,7 @@ def tile_netvlad_k_kernel(tc, x, conv_w, centroids, out):
         def finish_image(b):
             neg_wsum = work.tile([P, 1], F32, name="neg_wsum")
             nc.vector.tensor_scalar(
-                out=neg_wsum[:], in0=wsum_acc[b][:], scalar1=-1.0, scalar2=None, op0=ALU.mult
+                out=neg_wsum[:], in0=wsum_acc[b][:, 0:1], scalar1=-1.0, scalar2=None, op0=ALU.mult
             )
             result = work.tile([P, CHANNELS], F32, name="result")
             nc.vector.scalar_tensor_tensor(

@@ -28,7 +28,9 @@ ROUNDS = IMAGES * ROUNDS_PER_IMAGE
 SUM_COPIES = 96
 LOAD_AHEAD = 3
 
-VECTOR_PAIRS = 256
+RUN = 8
+RUNS = ROUND // RUN
+VECTOR_RUNS = 64
 
 FLOPS = 2 * 2 * IMAGES * POSITIONS * CHANNELS * CLUSTERS
 
@@ -97,10 +99,10 @@ def tile_netvlad_k_kernel(tc, x, conv_w, centroids, out):
 
         def regroup_by_channel(r):
             tile = work.tile([P, 2, PAIRS, PACK], BF16, align_bytes=64, name="by_channel")
-            src = x_sb[r][:].rearrange("q j (m e) -> q m j e", e=2)
-            dst = tile[:].rearrange("q e m j -> q m j e")
-            nc.vector.tensor_copy(out=dst[:, 0:VECTOR_PAIRS], in_=src[:, 0:VECTOR_PAIRS])
-            nc.scalar.copy(out=dst[:, VECTOR_PAIRS:PAIRS], in_=src[:, VECTOR_PAIRS:PAIRS])
+            src = x_sb[r][:].rearrange("q j (c m e) -> q c j m e", e=2, c=RUNS)
+            dst = tile[:].rearrange("q e (c m) j -> q c j m e", c=RUNS)
+            nc.vector.tensor_copy(out=dst[:, 0:VECTOR_RUNS], in_=src[:, 0:VECTOR_RUNS])
+            nc.scalar.copy(out=dst[:, VECTOR_RUNS:RUNS], in_=src[:, VECTOR_RUNS:RUNS])
             by_channel[r] = tile
 
         def quantise_by_channel(r):

@@ -26,11 +26,14 @@ PAIRS = ROUND // 2
 ROUNDS_PER_IMAGE = POSITIONS // ROUND
 ROUNDS = IMAGES * ROUNDS_PER_IMAGE
 SUM_COPIES = 96
-LOAD_AHEAD = 3
+LOAD_AHEAD = 5
 
 RUN = 8
 RUNS = ROUND // RUN
-VECTOR_RUNS = 64
+VECTOR_RUNS = 56
+GPSIMD_RUNS = 16
+SCALAR_END = RUNS - GPSIMD_RUNS
+GPSIMD_PAIR0 = SCALAR_END * RUN // 2
 
 FLOPS = 2 * 2 * IMAGES * POSITIONS * CHANNELS * CLUSTERS
 
@@ -43,6 +46,7 @@ def tile_netvlad_k_kernel(tc, x, conv_w, centroids, out):
     with ExitStack() as ctx:
         const = ctx.enter_context(tc.tile_pool(name="const", bufs=1))
         loads = ctx.enter_context(tc.tile_pool(name="loads", bufs=LOAD_AHEAD + 2))
+        grouped = ctx.enter_context(tc.tile_pool(name="grouped", bufs=2))
         work = ctx.enter_context(tc.tile_pool(name="work", bufs=3))
         sums = ctx.enter_context(tc.psum_pool(name="sums", bufs=1))
         logit_banks = ctx.enter_context(tc.psum_pool(name="logit_banks", bufs=PASSES))
@@ -97,13 +101,24 @@ def tile_netvlad_k_kernel(tc, x, conv_w, centroids, out):
             nc.sync.dma_start(out=tile[:], in_=x_rows[b, :, :, i * ROUND : (i + 1) * ROUND])
             x_sb[r] = tile
 
+        def regroup_on_gpsimd(r):
+            tile = grouped.tile([P, 2, PAIRS, PACK], BF16, align_bytes=64, name="by_channel")
+            nc.gpsimd.tensor_scalar(
+                out=tile[:, :, GPSIMD_PAIR0:PAIRS, :],
+                in0=x_sb[r][:].rearrange("q j (m e) -> q e m j", e=2)[:, :, GPSIMD_PAIR0:PAIRS],
+                scalar1=1.0,
+                scalar2=0.0,
+                op0=ALU.mult,
+                op1=ALU.add,
+            )
+            by_channel[r] = tile
+
         def regroup_by_channel(r):
-            tile = work.tile([P, 2, PAIRS, PACK], BF16, align_bytes=64, name="by_channel")
+            tile = by_channel[r]
             src = x_sb[r][:].rearrange("q j (c m e) -> q c j m e", e=2, c=RUNS)
             dst = tile[:].rearrange("q e (c m) j -> q c j m e", c=RUNS)
             nc.vector.tensor_copy(out=dst[:, 0:VECTOR_RUNS], in_=src[:, 0:VECTOR_RUNS])
-            nc.scalar.copy(out=dst[:, VECTOR_RUNS:RUNS], in_=src[:, VECTOR_RUNS:RUNS])
-            by_channel[r] = tile
+            nc.scalar.copy(out=dst[:, VECTOR_RUNS:SCALAR_END], in_=src[:, VECTOR_RUNS:SCALAR_END])
 
         def quantise_by_channel(r):
             codes = work.tile([P, ROUND], U32, align_bytes=64, name="xc_codes")
@@ -195,10 +210,13 @@ def tile_netvlad_k_kernel(tc, x, conv_w, centroids, out):
             expo[r] = tile
             inv_total[r] = total
 
-        def normalise(r):
+        def invert_totals(r):
             inv = work.tile([P, PASSES, PACK], F32, name="inv_total")
             nc.vector.reciprocal(out=inv[:], in_=inv_total[r][:])
             inv_total[r] = inv
+
+        def normalise(r):
+            inv = inv_total[r]
             tile = work.tile([P, PASSES, CLUSTERS, PACK], BF16, align_bytes=64, name="w_grouped")
             nc.vector.tensor_tensor(
                 out=tile[:],
@@ -270,29 +288,33 @@ def tile_netvlad_k_kernel(tc, x, conv_w, centroids, out):
             return 0 <= r < ROUNDS
 
         with tc.manual_schedule():
-            for s in range(-LOAD_AHEAD, ROUNDS + 1):
+            for s in range(-LOAD_AHEAD, ROUNDS + 2):
                 if is_round(s + LOAD_AHEAD):
                     load(s + LOAD_AHEAD)
                 if is_round(s + 1):
                     transpose_positions(s + 1)
+                    quantise_by_channel(s + 1)
+                if is_round(s + 3):
+                    regroup_on_gpsimd(s + 3)
                 if is_round(s):
                     row_max(s)
-                    exponentials(s)
-                if is_round(s + 1):
-                    quantise_by_channel(s + 1)
-                if is_round(s - 1):
-                    second_matmul(s - 1)
-                    if s % ROUNDS_PER_IMAGE == 0:
-                        finish_image(s // ROUNDS_PER_IMAGE - 1)
-                if is_round(s + 1):
-                    first_matmul(s + 1)
                 if is_round(s + 2):
                     regroup_by_channel(s + 2)
                 if is_round(s):
-                    normalise(s)
-                    sum_w(s)
+                    exponentials(s)
+                if is_round(s - 2):
+                    second_matmul(s - 2)
+                    if (s - 1) % ROUNDS_PER_IMAGE == 0:
+                        finish_image((s - 1) // ROUNDS_PER_IMAGE - 1)
+                if is_round(s - 1):
+                    sum_w(s - 1)
                 if is_round(s + 1):
+                    first_matmul(s + 1)
                     regroup_by_position(s + 1)
                 if is_round(s):
                     quantise_by_position(s)
-                    quantise_w(s)
+                    invert_totals(s)
+                if is_round(s - 1):
+                    quantise_w(s - 1)
+                if is_round(s):
+                    normalise(s)

@@ -30,8 +30,8 @@ LOAD_AHEAD = 5
 
 RUN = 8
 RUNS = ROUND // RUN
-VECTOR_RUNS = 56
-GPSIMD_RUNS = 16
+VECTOR_RUNS = 40
+GPSIMD_RUNS = 40
 SCALAR_END = RUNS - GPSIMD_RUNS
 GPSIMD_PAIR0 = SCALAR_END * RUN // 2
 
@@ -46,7 +46,6 @@ def tile_netvlad_k_kernel(tc, x, conv_w, centroids, out):
     with ExitStack() as ctx:
         const = ctx.enter_context(tc.tile_pool(name="const", bufs=1))
         loads = ctx.enter_context(tc.tile_pool(name="loads", bufs=LOAD_AHEAD + 2))
-        grouped = ctx.enter_context(tc.tile_pool(name="grouped", bufs=2))
         work = ctx.enter_context(tc.tile_pool(name="work", bufs=3))
         sums = ctx.enter_context(tc.psum_pool(name="sums", bufs=1))
         logit_banks = ctx.enter_context(tc.psum_pool(name="logit_banks", bufs=PASSES))
@@ -77,8 +76,9 @@ def tile_netvlad_k_kernel(tc, x, conv_w, centroids, out):
             in_=conv_grouped[:].rearrange("q k t -> q (k t)"),
         )
 
+        by_channel = const.tile([P, 2, 2, PAIRS, PACK], BF16, align_bytes=64)
+
         x_sb = {}
-        by_channel = {}
         xc_codes = {}
         xc_scales = {}
         flips = {}
@@ -89,6 +89,7 @@ def tile_netvlad_k_kernel(tc, x, conv_w, centroids, out):
         neg_max = {}
         expo = {}
         inv_total = {}
+        inv_psum = {}
         w_grouped = {}
         w_codes = {}
         w_scales = {}
@@ -101,35 +102,33 @@ def tile_netvlad_k_kernel(tc, x, conv_w, centroids, out):
             nc.sync.dma_start(out=tile[:], in_=x_rows[b, :, :, i * ROUND : (i + 1) * ROUND])
             x_sb[r] = tile
 
-        def regroup_on_gpsimd(r):
-            tile = grouped.tile([P, 2, PAIRS, PACK], BF16, align_bytes=64, name="by_channel")
+        def regroup_on_gpsimd(r, e):
             nc.gpsimd.tensor_scalar(
-                out=tile[:, :, GPSIMD_PAIR0:PAIRS, :],
-                in0=x_sb[r][:].rearrange("q j (m e) -> q e m j", e=2)[:, :, GPSIMD_PAIR0:PAIRS],
+                out=by_channel[:, r % 2, e, GPSIMD_PAIR0:PAIRS, :],
+                in0=x_sb[r][:].rearrange("q j (m e) -> q e m j", e=2)[:, e, GPSIMD_PAIR0:PAIRS],
                 scalar1=1.0,
                 scalar2=0.0,
                 op0=ALU.mult,
                 op1=ALU.add,
             )
-            by_channel[r] = tile
 
         def regroup_by_channel(r):
-            tile = by_channel[r]
             src = x_sb[r][:].rearrange("q j (c m e) -> q c j m e", e=2, c=RUNS)
-            dst = tile[:].rearrange("q e (c m) j -> q c j m e", c=RUNS)
+            dst = by_channel[:, r % 2].rearrange("q e (c m) j -> q c j m e", c=RUNS)
             nc.vector.tensor_copy(out=dst[:, 0:VECTOR_RUNS], in_=src[:, 0:VECTOR_RUNS])
             nc.scalar.copy(out=dst[:, VECTOR_RUNS:SCALAR_END], in_=src[:, VECTOR_RUNS:SCALAR_END])
 
-        def quantise_by_channel(r):
-            codes = work.tile([P, ROUND], U32, align_bytes=64, name="xc_codes")
-            scales = work.tile([P, ROUND], U8, align_bytes=64, name="xc_scales")
+        def quantise_by_channel(r, e):
+            if e == 0:
+                codes = work.tile([P, 2, PAIRS], U32, align_bytes=64, name="xc_codes")
+                scales = work.tile([P, 2, PAIRS], U8, align_bytes=64, name="xc_scales")
+                xc_codes[r] = codes
+                xc_scales[r] = scales
             nc.vector.quantize_mx(
-                out=codes[:].bitcast(FP8X4),
-                scales=scales[:],
-                in_=by_channel[r][:].rearrange("q e m j -> q (e m j)"),
+                out=xc_codes[r][:, e, :].bitcast(FP8X4),
+                scales=xc_scales[r][:, e, :],
+                in_=by_channel[:, r % 2, e].rearrange("q m j -> q (m j)"),
             )
-            xc_codes[r] = codes
-            xc_scales[r] = scales
 
         def transpose_positions(r):
             x_words = x_sb[r][:].bitcast(F32)
@@ -174,11 +173,11 @@ def tile_netvlad_k_kernel(tc, x, conv_w, centroids, out):
                 bank = logit_banks.tile([P, PACK, CLUSTERS], F32, name="logits")
                 for u in range(2):
                     for e in range(2):
-                        col0 = e * PAIRS + (2 * g + u) * P
+                        col0 = (2 * g + u) * P
                         nc.tensor.matmul_mx(
                             out=bank[:, 2 * u + e, :],
-                            lhsT=xc_codes[r][:, col0 : col0 + P].bitcast(FP8X4),
-                            lhsT_scale=xc_scales[r][:, col0 : col0 + P],
+                            lhsT=xc_codes[r][:, e, col0 : col0 + P].bitcast(FP8X4),
+                            lhsT_scale=xc_scales[r][:, e, col0 : col0 + P],
                             rhs=conv_codes[:].bitcast(FP8X4),
                             rhs_scale=conv_scales[:],
                             start=True,
@@ -215,13 +214,23 @@ def tile_netvlad_k_kernel(tc, x, conv_w, centroids, out):
             nc.vector.reciprocal(out=inv[:], in_=inv_total[r][:])
             inv_total[r] = inv
 
+        def inverses_to_psum(r):
+            bank = flip_banks.tile([P, 2, 2 * P], F32, tag="flip", name="inv_psum")
+            nc.tensor.matmul(
+                out=bank[:, 0, 0 : PASSES * PACK],
+                lhsT=identity[:],
+                rhs=inv_total[r][:].rearrange("p g t -> p (g t)"),
+                start=True,
+                stop=True,
+            )
+            inv_psum[r] = bank[:, 0, 0 : PASSES * PACK].rearrange("p (g t) -> p g t", t=PACK)
+
         def normalise(r):
-            inv = inv_total[r]
             tile = work.tile([P, PASSES, CLUSTERS, PACK], BF16, align_bytes=64, name="w_grouped")
             nc.vector.tensor_tensor(
                 out=tile[:],
                 in0=expo[r][:].rearrange("p g t k -> p g k t"),
-                in1=inv[:].unsqueeze(2).to_broadcast([P, PASSES, CLUSTERS, PACK]),
+                in1=inv_psum[r].unsqueeze(2).to_broadcast([P, PASSES, CLUSTERS, PACK]),
                 op=ALU.mult,
             )
             w_grouped[r] = tile
@@ -237,20 +246,19 @@ def tile_netvlad_k_kernel(tc, x, conv_w, centroids, out):
             w_codes[r] = codes
             w_scales[r] = scales
 
-        def sum_w(r):
+        def sum_w(r, g):
             b, i = divmod(r, ROUNDS_PER_IMAGE)
-            if i == 0:
+            if i == 0 and g == 0:
                 acc = sums.tile([P, SUM_COPIES], F32, name="wsum_acc")
                 wsum_acc[b] = acc
-            for g in range(PASSES):
-                for t in range(PACK):
-                    nc.tensor.matmul(
-                        out=wsum_acc[b][:],
-                        lhsT=expo[r][:, g, t, :],
-                        rhs=inv_total[r][:, g, t : t + 1].to_broadcast([P, SUM_COPIES]),
-                        start=(i == 0 and g == 0 and t == 0),
-                        stop=(i == ROUNDS_PER_IMAGE - 1 and g == PASSES - 1 and t == PACK - 1),
-                    )
+            for t in range(PACK):
+                nc.tensor.matmul(
+                    out=wsum_acc[b][:],
+                    lhsT=expo[r][:, g, t, :],
+                    rhs=inv_total[r][:, g, t : t + 1].to_broadcast([P, SUM_COPIES]),
+                    start=(i == 0 and g == 0 and t == 0),
+                    stop=(i == ROUNDS_PER_IMAGE - 1 and g == PASSES - 1 and t == PACK - 1),
+                )
 
         def second_matmul(r):
             b, i = divmod(r, ROUNDS_PER_IMAGE)
@@ -293,28 +301,33 @@ def tile_netvlad_k_kernel(tc, x, conv_w, centroids, out):
                     load(s + LOAD_AHEAD)
                 if is_round(s + 1):
                     transpose_positions(s + 1)
-                    quantise_by_channel(s + 1)
+                    quantise_by_channel(s + 1, 0)
                 if is_round(s + 3):
-                    regroup_on_gpsimd(s + 3)
+                    regroup_on_gpsimd(s + 3, 0)
                 if is_round(s):
                     row_max(s)
                 if is_round(s + 2):
                     regroup_by_channel(s + 2)
                 if is_round(s):
                     exponentials(s)
+                    quantise_by_position(s)
+                    invert_totals(s)
                 if is_round(s - 2):
                     second_matmul(s - 2)
                     if (s - 1) % ROUNDS_PER_IMAGE == 0:
                         finish_image((s - 1) // ROUNDS_PER_IMAGE - 1)
                 if is_round(s - 1):
-                    sum_w(s - 1)
+                    sum_w(s - 1, 0)
+                    quantise_w(s - 1)
+                if is_round(s + 1):
+                    regroup_by_position(s + 1)
+                    quantise_by_channel(s + 1, 1)
+                if is_round(s + 3):
+                    regroup_on_gpsimd(s + 3, 1)
+                if is_round(s):
+                    inverses_to_psum(s)
+                    normalise(s)
                 if is_round(s + 1):
                     first_matmul(s + 1)
-                    regroup_by_position(s + 1)
-                if is_round(s):
-                    quantise_by_position(s)
-                    invert_totals(s)
                 if is_round(s - 1):
-                    quantise_w(s - 1)
-                if is_round(s):
-                    normalise(s)
+                    sum_w(s - 1, 1)

@@ -30,8 +30,8 @@ LOAD_AHEAD = 5
 
 RUN = 8
 RUNS = ROUND // RUN
-VECTOR_RUNS = 40
-GPSIMD_RUNS = 40
+VECTOR_RUNS = 44
+GPSIMD_RUNS = 28
 SCALAR_END = RUNS - GPSIMD_RUNS
 GPSIMD_PAIR0 = SCALAR_END * RUN // 2
 

@@ -30,6 +30,7 @@ LOAD_AHEAD = 5
 
 RUN = 8
 RUNS = ROUND // RUN
+LINE = 4
 VECTOR_RUNS = 44
 GPSIMD_RUNS = 28
 SCALAR_END = RUNS - GPSIMD_RUNS
@@ -55,10 +56,9 @@ def tile_netvlad_k_kernel(tc, x, conv_w, centroids, out):
         make_identity(nc, identity[:])
 
         centroid_sb = const.tile([P, CHANNELS], BF16)
-        nc.scalar.dma_start(out=centroid_sb[:], in_=centroids)
 
         conv_sb = const.tile([P, CHANNELS], BF16)
-        nc.scalar.dma_start(out=conv_sb[:], in_=conv_w)
+        nc.sync.dma_start(out=conv_sb[:], in_=conv_w)
         conv_words = conv_sb[:].bitcast(F32).rearrange("k (q u) -> k u q", u=2)
         conv_flip = flip_banks.tile([P, 2, 2 * P], F32, tag="flip")
         for u in range(2):
@@ -99,7 +99,12 @@ def tile_netvlad_k_kernel(tc, x, conv_w, centroids, out):
         def load(r):
             b, i = divmod(r, ROUNDS_PER_IMAGE)
             tile = loads.tile([P, PACK, ROUND], BF16, name="x_sb")
-            nc.sync.dma_start(out=tile[:], in_=x_rows[b, :, :, i * ROUND : (i + 1) * ROUND])
+            edges = [0, VECTOR_RUNS * RUN, SCALAR_END * RUN, ROUND] if r == 0 else [0, ROUND]
+            for lo, hi in zip(edges, edges[1:]):
+                nc.sync.dma_start(
+                    out=tile[:, :, lo:hi],
+                    in_=x_rows[b, :, :, i * ROUND + lo : i * ROUND + hi],
+                )
             x_sb[r] = tile
 
         def regroup_on_gpsimd(r, e):
@@ -227,12 +232,16 @@ def tile_netvlad_k_kernel(tc, x, conv_w, centroids, out):
 
         def normalise(r):
             tile = work.tile([P, PASSES, CLUSTERS, PACK], BF16, align_bytes=64, name="w_grouped")
-            nc.vector.tensor_tensor(
-                out=tile[:],
-                in0=expo[r][:].rearrange("p g t k -> p g k t"),
-                in1=inv_psum[r].unsqueeze(2).to_broadcast([P, PASSES, CLUSTERS, PACK]),
-                op=ALU.mult,
-            )
+            for g in range(PASSES):
+                nc.vector.tensor_tensor(
+                    out=tile[:, g].rearrange("p (c k) t -> p c t k", k=LINE),
+                    in0=expo[r][:, g].rearrange("p t (c k) -> p c t k", k=LINE),
+                    in1=inv_psum[r][:, g]
+                    .unsqueeze(1)
+                    .unsqueeze(3)
+                    .to_broadcast([P, CLUSTERS // LINE, PACK, LINE]),
+                    op=ALU.mult,
+                )
             w_grouped[r] = tile
 
         def quantise_w(r):
@@ -299,6 +308,8 @@ def tile_netvlad_k_kernel(tc, x, conv_w, centroids, out):
             for s in range(-LOAD_AHEAD, ROUNDS + 2):
                 if is_round(s + LOAD_AHEAD):
                     load(s + LOAD_AHEAD)
+                if s == 0:
+                    nc.sync.dma_start(out=centroid_sb[:], in_=centroids)
                 if is_round(s + 1):
                     transpose_positions(s + 1)
                     quantise_by_channel(s + 1, 0)

@@ -31,8 +31,8 @@ LOAD_AHEAD = 5
 RUN = 8
 RUNS = ROUND // RUN
 LINE = 4
-VECTOR_RUNS = 44
-GPSIMD_RUNS = 28
+VECTOR_RUNS = 42
+GPSIMD_RUNS = 32
 SCALAR_END = RUNS - GPSIMD_RUNS
 GPSIMD_PAIR0 = SCALAR_END * RUN // 2
 
@@ -54,6 +54,8 @@ def tile_netvlad_k_kernel(tc, x, conv_w, centroids, out):
 
         identity = const.tile([P, P], F32)
         make_identity(nc, identity[:])
+        table_load = const.tile([P, 1], F32)
+        nc.scalar.activation(out=table_load[:], in_=identity[:, 0:1], func=ACT.Exp)
 
         centroid_sb = const.tile([P, CHANNELS], BF16)
 
@@ -99,12 +101,7 @@ def tile_netvlad_k_kernel(tc, x, conv_w, centroids, out):
         def load(r):
             b, i = divmod(r, ROUNDS_PER_IMAGE)
             tile = loads.tile([P, PACK, ROUND], BF16, name="x_sb")
-            edges = [0, VECTOR_RUNS * RUN, SCALAR_END * RUN, ROUND] if r == 0 else [0, ROUND]
-            for lo, hi in zip(edges, edges[1:]):
-                nc.sync.dma_start(
-                    out=tile[:, :, lo:hi],
-                    in_=x_rows[b, :, :, i * ROUND + lo : i * ROUND + hi],
-                )
+            nc.sync.dma_start(out=tile[:], in_=x_rows[b, :, :, i * ROUND : (i + 1) * ROUND])
             x_sb[r] = tile
 
         def regroup_on_gpsimd(r, e):
@@ -335,10 +332,12 @@ def tile_netvlad_k_kernel(tc, x, conv_w, centroids, out):
                     quantise_by_channel(s + 1, 1)
                 if is_round(s + 3):
                     regroup_on_gpsimd(s + 3, 1)
+                if s in (ROUNDS - 1, ROUNDS):
+                    sum_w(s - 1, 1)
                 if is_round(s):
                     inverses_to_psum(s)
                     normalise(s)
                 if is_round(s + 1):
                     first_matmul(s + 1)
-                if is_round(s - 1):
-                    sum_w(s - 1, 1)
+                    if is_round(s - 1):
+                        sum_w(s - 1, 1)

@@ -31,10 +31,9 @@ LOAD_AHEAD = 5
 RUN = 8
 RUNS = ROUND // RUN
 LINE = 4
-VECTOR_RUNS = 42
-GPSIMD_RUNS = 32
+VECTOR_RUNS = 40
+GPSIMD_RUNS = 40
 SCALAR_END = RUNS - GPSIMD_RUNS
-GPSIMD_PAIR0 = SCALAR_END * RUN // 2
 
 FLOPS = 2 * 2 * IMAGES * POSITIONS * CHANNELS * CLUSTERS
 
@@ -106,8 +105,8 @@ def tile_netvlad_k_kernel(tc, x, conv_w, centroids, out):
 
         def regroup_on_gpsimd(r, e):
             nc.gpsimd.tensor_scalar(
-                out=by_channel[:, r % 2, e, GPSIMD_PAIR0:PAIRS, :],
-                in0=x_sb[r][:].rearrange("q j (m e) -> q e m j", e=2)[:, e, GPSIMD_PAIR0:PAIRS],
+                out=by_channel[:, r % 2, e].rearrange("q (c m) j -> q c j m", c=RUNS)[:, SCALAR_END:],
+                in0=x_sb[r][:].rearrange("q j (c m e) -> q e c j m", e=2, c=RUNS)[:, e, SCALAR_END:],
                 scalar1=1.0,
                 scalar2=0.0,
                 op0=ALU.mult,

@@ -31,8 +31,8 @@ LOAD_AHEAD = 5
 RUN = 8
 RUNS = ROUND // RUN
 LINE = 4
-VECTOR_RUNS = 40
-GPSIMD_RUNS = 40
+VECTOR_RUNS = 34
+GPSIMD_RUNS = 44
 SCALAR_END = RUNS - GPSIMD_RUNS
 
 FLOPS = 2 * 2 * IMAGES * POSITIONS * CHANNELS * CLUSTERS
@@ -103,33 +103,40 @@ def tile_netvlad_k_kernel(tc, x, conv_w, centroids, out):
             nc.sync.dma_start(out=tile[:], in_=x_rows[b, :, :, i * ROUND : (i + 1) * ROUND])
             x_sb[r] = tile
 
-        def regroup_on_gpsimd(r, e):
-            nc.gpsimd.tensor_scalar(
-                out=by_channel[:, r % 2, e].rearrange("q (c m) j -> q c j m", c=RUNS)[:, SCALAR_END:],
-                in0=x_sb[r][:].rearrange("q j (c m e) -> q e c j m", e=2, c=RUNS)[:, e, SCALAR_END:],
-                scalar1=1.0,
-                scalar2=0.0,
-                op0=ALU.mult,
-                op1=ALU.add,
-            )
+        def regroup_on_gpsimd(r):
+            for e in range(2):
+                nc.gpsimd.tensor_scalar(
+                    out=by_channel[:, r % 2, e].rearrange("q (c m) j -> q c j m", c=RUNS)[:, SCALAR_END:],
+                    in0=x_sb[r][:].rearrange("q j (c m e) -> q e c j m", e=2, c=RUNS)[:, e, SCALAR_END:],
+                    scalar1=1.0,
+                    scalar2=0.0,
+                    op0=ALU.mult,
+                    op1=ALU.add,
+                )
 
-        def regroup_by_channel(r):
+        def regroup_views(r):
             src = x_sb[r][:].rearrange("q j (c m e) -> q c j m e", e=2, c=RUNS)
             dst = by_channel[:, r % 2].rearrange("q e (c m) j -> q c j m e", c=RUNS)
+            return dst, src
+
+        def regroup_on_vector(r):
+            dst, src = regroup_views(r)
             nc.vector.tensor_copy(out=dst[:, 0:VECTOR_RUNS], in_=src[:, 0:VECTOR_RUNS])
+
+        def regroup_on_scalar(r):
+            dst, src = regroup_views(r)
             nc.scalar.copy(out=dst[:, VECTOR_RUNS:SCALAR_END], in_=src[:, VECTOR_RUNS:SCALAR_END])
 
-        def quantise_by_channel(r, e):
-            if e == 0:
-                codes = work.tile([P, 2, PAIRS], U32, align_bytes=64, name="xc_codes")
-                scales = work.tile([P, 2, PAIRS], U8, align_bytes=64, name="xc_scales")
-                xc_codes[r] = codes
-                xc_scales[r] = scales
+        def quantise_by_channel(r):
+            codes = work.tile([P, 2, PAIRS], U32, align_bytes=64, name="xc_codes")
+            scales = work.tile([P, 2, PAIRS], U8, align_bytes=64, name="xc_scales")
             nc.vector.quantize_mx(
-                out=xc_codes[r][:, e, :].bitcast(FP8X4),
-                scales=xc_scales[r][:, e, :],
-                in_=by_channel[:, r % 2, e].rearrange("q m j -> q (m j)"),
+                out=codes[:].rearrange("q e m -> q (e m)").bitcast(FP8X4),
+                scales=scales[:].rearrange("q e m -> q (e m)"),
+                in_=by_channel[:, r % 2].rearrange("q e m j -> q (e m j)"),
             )
+            xc_codes[r] = codes
+            xc_scales[r] = scales
 
         def transpose_positions(r):
             x_words = x_sb[r][:].bitcast(F32)
@@ -251,19 +258,20 @@ def tile_netvlad_k_kernel(tc, x, conv_w, centroids, out):
             w_codes[r] = codes
             w_scales[r] = scales
 
-        def sum_w(r, g):
+        def sum_w(r):
             b, i = divmod(r, ROUNDS_PER_IMAGE)
-            if i == 0 and g == 0:
+            if i == 0:
                 acc = sums.tile([P, SUM_COPIES], F32, name="wsum_acc")
                 wsum_acc[b] = acc
-            for t in range(PACK):
-                nc.tensor.matmul(
-                    out=wsum_acc[b][:],
-                    lhsT=expo[r][:, g, t, :],
-                    rhs=inv_total[r][:, g, t : t + 1].to_broadcast([P, SUM_COPIES]),
-                    start=(i == 0 and g == 0 and t == 0),
-                    stop=(i == ROUNDS_PER_IMAGE - 1 and g == PASSES - 1 and t == PACK - 1),
-                )
+            for g in range(PASSES):
+                for t in range(PACK):
+                    nc.tensor.matmul(
+                        out=wsum_acc[b][:],
+                        lhsT=expo[r][:, g, t, :],
+                        rhs=inv_total[r][:, g, t : t + 1].to_broadcast([P, SUM_COPIES]),
+                        start=(i == 0 and g == 0 and t == 0),
+                        stop=(i == ROUNDS_PER_IMAGE - 1 and g == PASSES - 1 and t == PACK - 1),
+                    )
 
         def second_matmul(r):
             b, i = divmod(r, ROUNDS_PER_IMAGE)
@@ -301,42 +309,39 @@ def tile_netvlad_k_kernel(tc, x, conv_w, centroids, out):
             return 0 <= r < ROUNDS
 
         with tc.manual_schedule():
-            for s in range(-LOAD_AHEAD, ROUNDS + 2):
+            for s in range(-LOAD_AHEAD, ROUNDS + 1):
                 if is_round(s + LOAD_AHEAD):
                     load(s + LOAD_AHEAD)
                 if s == 0:
                     nc.sync.dma_start(out=centroid_sb[:], in_=centroids)
                 if is_round(s + 1):
-                    transpose_positions(s + 1)
-                    quantise_by_channel(s + 1, 0)
+                    quantise_by_channel(s + 1)
                 if is_round(s + 3):
-                    regroup_on_gpsimd(s + 3, 0)
+                    regroup_on_gpsimd(s + 3)
                 if is_round(s):
-                    row_max(s)
-                if is_round(s + 2):
-                    regroup_by_channel(s + 2)
-                if is_round(s):
-                    exponentials(s)
-                    quantise_by_position(s)
-                    invert_totals(s)
-                if is_round(s - 2):
-                    second_matmul(s - 2)
-                    if (s - 1) % ROUNDS_PER_IMAGE == 0:
-                        finish_image((s - 1) // ROUNDS_PER_IMAGE - 1)
-                if is_round(s - 1):
-                    sum_w(s - 1, 0)
-                    quantise_w(s - 1)
-                if is_round(s + 1):
-                    regroup_by_position(s + 1)
-                    quantise_by_channel(s + 1, 1)
-                if is_round(s + 3):
-                    regroup_on_gpsimd(s + 3, 1)
-                if s in (ROUNDS - 1, ROUNDS):
-                    sum_w(s - 1, 1)
-                if is_round(s):
-                    inverses_to_psum(s)
                     normalise(s)
                 if is_round(s + 1):
                     first_matmul(s + 1)
-                    if is_round(s - 1):
-                        sum_w(s - 1, 1)
+                    row_max(s + 1)
+                if is_round(s - 1) and s % ROUNDS_PER_IMAGE == 0:
+                    finish_image(s // ROUNDS_PER_IMAGE - 1)
+                if is_round(s + 3):
+                    regroup_on_vector(s + 3)
+                if is_round(s + 1):
+                    exponentials(s + 1)
+                if is_round(s + 2):
+                    transpose_positions(s + 2)
+                if is_round(s + 1):
+                    quantise_by_position(s + 1)
+                if is_round(s):
+                    sum_w(s)
+                    quantise_w(s)
+                    second_matmul(s)
+                if is_round(s + 1):
+                    invert_totals(s + 1)
+                if is_round(s + 2):
+                    regroup_by_position(s + 2)
+                if is_round(s + 3):
+                    regroup_on_scalar(s + 3)
+                if is_round(s + 1):
+                    inverses_to_psum(s + 1)

@@ -60,22 +60,8 @@ def tile_netvlad_k_kernel(tc, x, conv_w, centroids, out):
 
         conv_sb = const.tile([P, CHANNELS], BF16)
         nc.sync.dma_start(out=conv_sb[:], in_=conv_w)
-        conv_words = conv_sb[:].bitcast(F32).rearrange("k (q u) -> k u q", u=2)
-        conv_flip = flip_banks.tile([P, 2, 2 * P], F32, tag="flip")
-        for u in range(2):
-            nc.tensor.transpose(conv_flip[:, u, 0:P], conv_words[:, u, :], identity[:])
-        conv_grouped = const.tile([P, CLUSTERS, PACK], BF16, align_bytes=64)
-        nc.vector.tensor_copy(
-            out=conv_grouped[:].bitcast(F32),
-            in_=conv_flip[:, :, 0:P].rearrange("q u k -> q k u"),
-        )
         conv_codes = const.tile([P, CLUSTERS], U32, align_bytes=64)
         conv_scales = const.tile([P, CLUSTERS], U8, align_bytes=64)
-        nc.vector.quantize_mx(
-            out=conv_codes[:].bitcast(FP8X4),
-            scales=conv_scales[:],
-            in_=conv_grouped[:].rearrange("q k t -> q (k t)"),
-        )
 
         by_channel = const.tile([P, 2, 2, PAIRS, PACK], BF16, align_bytes=64)
 
@@ -96,6 +82,22 @@ def tile_netvlad_k_kernel(tc, x, conv_w, centroids, out):
         w_scales = {}
         vlad_acc = {}
         wsum_acc = {}
+
+        def quantise_conv():
+            conv_words = conv_sb[:].bitcast(F32).rearrange("k (q u) -> k u q", u=2)
+            conv_flip = flip_banks.tile([P, 2, 2 * P], F32, tag="flip")
+            for u in range(2):
+                nc.tensor.transpose(conv_flip[:, u, 0:P], conv_words[:, u, :], identity[:])
+            conv_grouped = const.tile([P, CLUSTERS, PACK], BF16, align_bytes=64)
+            nc.vector.tensor_copy(
+                out=conv_grouped[:].bitcast(F32),
+                in_=conv_flip[:, :, 0:P].rearrange("q u k -> q k u"),
+            )
+            nc.vector.quantize_mx(
+                out=conv_codes[:].bitcast(FP8X4),
+                scales=conv_scales[:],
+                in_=conv_grouped[:].rearrange("q k t -> q (k t)"),
+            )
 
         def load(r):
             b, i = divmod(r, ROUNDS_PER_IMAGE)
@@ -122,6 +124,8 @@ def tile_netvlad_k_kernel(tc, x, conv_w, centroids, out):
         def regroup_on_vector(r):
             dst, src = regroup_views(r)
             nc.vector.tensor_copy(out=dst[:, 0:VECTOR_RUNS], in_=src[:, 0:VECTOR_RUNS])
+            if r == 0:
+                nc.vector.tensor_copy(out=dst[:, SCALAR_END:RUNS], in_=src[:, SCALAR_END:RUNS])
 
         def regroup_on_scalar(r):
             dst, src = regroup_views(r)
@@ -295,20 +299,24 @@ def tile_netvlad_k_kernel(tc, x, conv_w, centroids, out):
                 out=neg_wsum[:], in0=wsum_acc[b][:, 0:1], scalar1=-1.0, scalar2=None, op0=ALU.mult
             )
             result = work.tile([P, CHANNELS], F32, name="result")
-            nc.vector.scalar_tensor_tensor(
-                out=result[:],
-                in0=centroid_sb[:],
-                scalar=neg_wsum[:, 0:1],
-                in1=vlad_acc[b][:].rearrange("k (j q) -> k q j", j=PACK),
-                op0=ALU.mult,
-                op1=ALU.add,
-            )
-            nc.sync.dma_start(out=out_rows[b], in_=result[:])
+            by_row = vlad_acc[b][:].rearrange("k (j q) -> k q j", j=PACK)
+            for h in range(2):
+                half = slice(h * CHANNELS // 2, (h + 1) * CHANNELS // 2)
+                nc.vector.scalar_tensor_tensor(
+                    out=result[:, half],
+                    in0=centroid_sb[:, half],
+                    scalar=neg_wsum[:, 0:1],
+                    in1=by_row[:, h * P // 2 : (h + 1) * P // 2],
+                    op0=ALU.mult,
+                    op1=ALU.add,
+                )
+                nc.sync.dma_start(out=out_rows[b][:, half], in_=result[:, half])
 
         def is_round(r):
             return 0 <= r < ROUNDS
 
         with tc.manual_schedule():
+            quantise_conv()
             for s in range(-LOAD_AHEAD, ROUNDS + 1):
                 if is_round(s + LOAD_AHEAD):
                     load(s + LOAD_AHEAD)
@@ -316,8 +324,10 @@ def tile_netvlad_k_kernel(tc, x, conv_w, centroids, out):
                     nc.sync.dma_start(out=centroid_sb[:], in_=centroids)
                 if is_round(s + 1):
                     quantise_by_channel(s + 1)
-                if is_round(s + 3):
+                if is_round(s + 3) and s + 3 > 0:
                     regroup_on_gpsimd(s + 3)
+                if s == -1:
+                    regroup_on_vector(1)
                 if is_round(s):
                     normalise(s)
                 if is_round(s + 1):
@@ -325,7 +335,7 @@ def tile_netvlad_k_kernel(tc, x, conv_w, centroids, out):
                     row_max(s + 1)
                 if is_round(s - 1) and s % ROUNDS_PER_IMAGE == 0:
                     finish_image(s // ROUNDS_PER_IMAGE - 1)
-                if is_round(s + 3):
+                if is_round(s + 3) and s != -2:
                     regroup_on_vector(s + 3)
                 if is_round(s + 1):
                     exponentials(s + 1)

from contextlib import ExitStack

import concourse.mybir as mybir
from concourse.masks import make_identity

F32 = mybir.dt.float32
BF16 = mybir.dt.bfloat16
U32 = mybir.dt.uint32
U8 = mybir.dt.uint8
FP8X4 = mybir.dt.float8_e4m3fn_x4
ALU = mybir.AluOpType
ACT = mybir.ActivationFunctionType
AXIS = mybir.AxisListType

P = 128
PACK = 4
IMAGES = 2
CHANNELS = 512
POSITIONS = 16384
CLUSTERS = 128

PASS = P * PACK
ROUND = 2 * PASS
PASSES = ROUND // PASS
PAIRS = ROUND // 2
ROUNDS_PER_IMAGE = POSITIONS // ROUND
ROUNDS = IMAGES * ROUNDS_PER_IMAGE
SUM_COPIES = 96
LOAD_AHEAD = 5

RUN = 8
RUNS = ROUND // RUN
LINE = 4
VECTOR_RUNS = 34
GPSIMD_RUNS = 44
SCALAR_END = RUNS - GPSIMD_RUNS

FLOPS = 2 * 2 * IMAGES * POSITIONS * CHANNELS * CLUSTERS


def tile_netvlad_k_kernel(tc, x, conv_w, centroids, out):
    nc = tc.nc
    x_rows = x.rearrange("b (q j) h w -> b q j (h w)", j=PACK)
    out_rows = out.rearrange("b (k c) -> b k c", c=CHANNELS)

    with ExitStack() as ctx:
        const = ctx.enter_context(tc.tile_pool(name="const", bufs=1))
        loads = ctx.enter_context(tc.tile_pool(name="loads", bufs=LOAD_AHEAD + 2))
        work = ctx.enter_context(tc.tile_pool(name="work", bufs=3))
        sums = ctx.enter_context(tc.psum_pool(name="sums", bufs=1))
        logit_banks = ctx.enter_context(tc.psum_pool(name="logit_banks", bufs=PASSES))
        flip_banks = ctx.enter_context(tc.psum_pool(name="flip_banks", bufs=2 * PASSES))

        identity = const.tile([P, P], F32)
        make_identity(nc, identity[:])
        table_load = const.tile([P, 1], F32)
        nc.scalar.activation(out=table_load[:], in_=identity[:, 0:1], func=ACT.Exp)

        centroid_sb = const.tile([P, CHANNELS], BF16)

        conv_sb = const.tile([P, CHANNELS], BF16)
        nc.sync.dma_start(out=conv_sb[:], in_=conv_w)
        conv_codes = const.tile([P, CLUSTERS], U32, align_bytes=64)
        conv_scales = const.tile([P, CLUSTERS], U8, align_bytes=64)

        by_channel = const.tile([P, 2, 2, PAIRS, PACK], BF16, align_bytes=64)

        x_sb = {}
        xc_codes = {}
        xc_scales = {}
        flips = {}
        by_position = {}
        xp_codes = {}
        xp_scales = {}
        logits = {}
        neg_max = {}
        expo = {}
        inv_total = {}
        inv_psum = {}
        w_grouped = {}
        w_codes = {}
        w_scales = {}
        vlad_acc = {}
        wsum_acc = {}

        def quantise_conv():
            conv_words = conv_sb[:].bitcast(F32).rearrange("k (q u) -> k u q", u=2)
            conv_flip = flip_banks.tile([P, 2, 2 * P], F32, tag="flip")
            for u in range(2):
                nc.tensor.transpose(conv_flip[:, u, 0:P], conv_words[:, u, :], identity[:])
            conv_grouped = const.tile([P, CLUSTERS, PACK], BF16, align_bytes=64)
            nc.vector.tensor_copy(
                out=conv_grouped[:].bitcast(F32),
                in_=conv_flip[:, :, 0:P].rearrange("q u k -> q k u"),
            )
            nc.vector.quantize_mx(
                out=conv_codes[:].bitcast(FP8X4),
                scales=conv_scales[:],
                in_=conv_grouped[:].rearrange("q k t -> q (k t)"),
            )

        def load(r):
            b, i = divmod(r, ROUNDS_PER_IMAGE)
            tile = loads.tile([P, PACK, ROUND], BF16, name="x_sb")
            nc.sync.dma_start(out=tile[:], in_=x_rows[b, :, :, i * ROUND : (i + 1) * ROUND])
            x_sb[r] = tile

        def regroup_on_gpsimd(r):
            for e in range(2):
                nc.gpsimd.tensor_scalar(
                    out=by_channel[:, r % 2, e].rearrange("q (c m) j -> q c j m", c=RUNS)[:, SCALAR_END:],
                    in0=x_sb[r][:].rearrange("q j (c m e) -> q e c j m", e=2, c=RUNS)[:, e, SCALAR_END:],
                    scalar1=1.0,
                    scalar2=0.0,
                    op0=ALU.mult,
                    op1=ALU.add,
                )

        def regroup_views(r):
            src = x_sb[r][:].rearrange("q j (c m e) -> q c j m e", e=2, c=RUNS)
            dst = by_channel[:, r % 2].rearrange("q e (c m) j -> q c j m e", c=RUNS)
            return dst, src

        def regroup_on_vector(r):
            dst, src = regroup_views(r)
            nc.vector.tensor_copy(out=dst[:, 0:VECTOR_RUNS], in_=src[:, 0:VECTOR_RUNS])
            if r == 0:
                nc.vector.tensor_copy(out=dst[:, SCALAR_END:RUNS], in_=src[:, SCALAR_END:RUNS])

        def regroup_on_scalar(r):
            dst, src = regroup_views(r)
            nc.scalar.copy(out=dst[:, VECTOR_RUNS:SCALAR_END], in_=src[:, VECTOR_RUNS:SCALAR_END])

        def quantise_by_channel(r):
            codes = work.tile([P, 2, PAIRS], U32, align_bytes=64, name="xc_codes")
            scales = work.tile([P, 2, PAIRS], U8, align_bytes=64, name="xc_scales")
            nc.vector.quantize_mx(
                out=codes[:].rearrange("q e m -> q (e m)").bitcast(FP8X4),
                scales=scales[:].rearrange("q e m -> q (e m)"),
                in_=by_channel[:, r % 2].rearrange("q e m j -> q (e m j)"),
            )
            xc_codes[r] = codes
            xc_scales[r] = scales

        def transpose_positions(r):
            x_words = x_sb[r][:].bitcast(F32)
            flips[r] = []
            for g in range(PASSES):
                for jj in range(PACK // 2):
                    flip = flip_banks.tile([P, 2, 2 * P], F32, tag="flip", name="flip")
                    for u in range(2):
                        for j2 in range(2):
                            word0 = (2 * g + u) * P
                            nc.tensor.transpose(
                                flip[:, u, j2 * P : (j2 + 1) * P],
                                x_words[:, 2 * jj + j2, word0 : word0 + P],
                                identity[:],
                            )
                    flips[r].append(flip)

        def regroup_by_position(r):
            tile = work.tile([P, PASSES, CHANNELS, PACK], BF16, align_bytes=64, name="by_position")
            for g in range(PASSES):
                for jj in range(PACK // 2):
                    nc.scalar.copy(
                        out=tile[:, g, jj * 2 * P : (jj + 1) * 2 * P, :].bitcast(F32),
                        in_=flips[r][g * (PACK // 2) + jj][:].rearrange("p u c -> p c u"),
                    )
            by_position[r] = tile

        def quantise_by_position(r):
            codes = work.tile([P, PASSES, CHANNELS], U32, align_bytes=64, name="xp_codes")
            scales = work.tile([P, PASSES, CHANNELS], U8, align_bytes=64, name="xp_scales")
            nc.vector.quantize_mx(
                out=codes[:].rearrange("p g c -> p (g c)").bitcast(FP8X4),
                scales=scales[:].rearrange("p g c -> p (g c)"),
                in_=by_position[r][:].rearrange("p g c t -> p (g c t)"),
            )
            xp_codes[r] = codes
            xp_scales[r] = scales

        def first_matmul(r):
            logits[r] = []
            for g in range(PASSES):
                bank = logit_banks.tile([P, PACK, CLUSTERS], F32, name="logits")
                for u in range(2):
                    for e in range(2):
                        col0 = (2 * g + u) * P
                        nc.tensor.matmul_mx(
                            out=bank[:, 2 * u + e, :],
                            lhsT=xc_codes[r][:, e, col0 : col0 + P].bitcast(FP8X4),
                            lhsT_scale=xc_scales[r][:, e, col0 : col0 + P],
                            rhs=conv_codes[:].bitcast(FP8X4),
                            rhs_scale=conv_scales[:],
                            start=True,
                            stop=True,
                        )
                logits[r].append(bank)

        def row_max(r):
            tile = work.tile([P, PASSES, PACK], F32, name="neg_max")
            for g in range(PASSES):
                nc.vector.tensor_reduce(
                    out=tile[:, g, :], in_=logits[r][g][:], axis=AXIS.X, op=ALU.max, negate=True
                )
            neg_max[r] = tile

        def exponentials(r):
            tile = work.tile([P, PASSES, PACK, CLUSTERS], F32, name="expo")
            total = work.tile([P, PASSES, PACK], F32, name="total")
            for g in range(PASSES):
                for t in range(PACK):
                    nc.scalar.activation(
                        out=tile[:, g, t, :],
                        in_=logits[r][g][:, t, :],
                        func=ACT.Exp,
                        bias=neg_max[r][:, g, t : t + 1],
                        scale=1.0,
                        accum_out=total[:, g, t : t + 1],
                    )
            expo[r] = tile
            inv_total[r] = total

        def invert_totals(r):
            inv = work.tile([P, PASSES, PACK], F32, name="inv_total")
            nc.vector.reciprocal(out=inv[:], in_=inv_total[r][:])
            inv_total[r] = inv

        def inverses_to_psum(r):
            bank = flip_banks.tile([P, 2, 2 * P], F32, tag="flip", name="inv_psum")
            nc.tensor.matmul(
                out=bank[:, 0, 0 : PASSES * PACK],
                lhsT=identity[:],
                rhs=inv_total[r][:].rearrange("p g t -> p (g t)"),
                start=True,
                stop=True,
            )
            inv_psum[r] = bank[:, 0, 0 : PASSES * PACK].rearrange("p (g t) -> p g t", t=PACK)

        def normalise(r):
            tile = work.tile([P, PASSES, CLUSTERS, PACK], BF16, align_bytes=64, name="w_grouped")
            for g in range(PASSES):
                nc.vector.tensor_tensor(
                    out=tile[:, g].rearrange("p (c k) t -> p c t k", k=LINE),
                    in0=expo[r][:, g].rearrange("p t (c k) -> p c t k", k=LINE),
                    in1=inv_psum[r][:, g]
                    .unsqueeze(1)
                    .unsqueeze(3)
                    .to_broadcast([P, CLUSTERS // LINE, PACK, LINE]),
                    op=ALU.mult,
                )
            w_grouped[r] = tile

        def quantise_w(r):
            codes = work.tile([P, PASSES, CLUSTERS], U32, align_bytes=64, name="w_codes")
            scales = work.tile([P, PASSES, CLUSTERS], U8, align_bytes=64, name="w_scales")
            nc.vector.quantize_mx(
                out=codes[:].rearrange("p g k -> p (g k)").bitcast(FP8X4),
                scales=scales[:].rearrange("p g k -> p (g k)"),
                in_=w_grouped[r][:].rearrange("p g k t -> p (g k t)"),
            )
            w_codes[r] = codes
            w_scales[r] = scales

        def sum_w(r):
            b, i = divmod(r, ROUNDS_PER_IMAGE)
            if i == 0:
                acc = sums.tile([P, SUM_COPIES], F32, name="wsum_acc")
                wsum_acc[b] = acc
            for g in range(PASSES):
                for t in range(PACK):
                    nc.tensor.matmul(
                        out=wsum_acc[b][:],
                        lhsT=expo[r][:, g, t, :],
                        rhs=inv_total[r][:, g, t : t + 1].to_broadcast([P, SUM_COPIES]),
                        start=(i == 0 and g == 0 and t == 0),
                        stop=(i == ROUNDS_PER_IMAGE - 1 and g == PASSES - 1 and t == PACK - 1),
                    )

        def second_matmul(r):
            b, i = divmod(r, ROUNDS_PER_IMAGE)
            if i == 0:
                acc = sums.tile([P, CHANNELS], F32, name="vlad_acc")
                vlad_acc[b] = acc
            for g in range(PASSES):
                nc.tensor.matmul_mx(
                    out=vlad_acc[b][:],
                    lhsT=w_codes[r][:, g, :].bitcast(FP8X4),
                    lhsT_scale=w_scales[r][:, g, :],
                    rhs=xp_codes[r][:, g, :].bitcast(FP8X4),
                    rhs_scale=xp_scales[r][:, g, :],
                    start=(i == 0 and g == 0),
                    stop=(i == ROUNDS_PER_IMAGE - 1 and g == PASSES - 1),
                )

        def finish_image(b):
            neg_wsum = work.tile([P, 1], F32, name="neg_wsum")
            nc.vector.tensor_scalar(
                out=neg_wsum[:], in0=wsum_acc[b][:, 0:1], scalar1=-1.0, scalar2=None, op0=ALU.mult
            )
            result = work.tile([P, CHANNELS], F32, name="result")
            by_row = vlad_acc[b][:].rearrange("k (j q) -> k q j", j=PACK)
            for h in range(2):
                half = slice(h * CHANNELS // 2, (h + 1) * CHANNELS // 2)
                nc.vector.scalar_tensor_tensor(
                    out=result[:, half],
                    in0=centroid_sb[:, half],
                    scalar=neg_wsum[:, 0:1],
                    in1=by_row[:, h * P // 2 : (h + 1) * P // 2],
                    op0=ALU.mult,
                    op1=ALU.add,
                )
                nc.sync.dma_start(out=out_rows[b][:, half], in_=result[:, half])

        def is_round(r):
            return 0 <= r < ROUNDS

        with tc.manual_schedule():
            quantise_conv()
            for s in range(-LOAD_AHEAD, ROUNDS + 1):
                if is_round(s + LOAD_AHEAD):
                    load(s + LOAD_AHEAD)
                if s == 0:
                    nc.sync.dma_start(out=centroid_sb[:], in_=centroids)
                if is_round(s + 1):
                    quantise_by_channel(s + 1)
                if is_round(s + 3) and s + 3 > 0:
                    regroup_on_gpsimd(s + 3)
                if s == -1:
                    regroup_on_vector(1)
                if is_round(s):
                    normalise(s)
                if is_round(s + 1):
                    first_matmul(s + 1)
                    row_max(s + 1)
                if is_round(s - 1) and s % ROUNDS_PER_IMAGE == 0:
                    finish_image(s // ROUNDS_PER_IMAGE - 1)
                if is_round(s + 3) and s != -2:
                    regroup_on_vector(s + 3)
                if is_round(s + 1):
                    exponentials(s + 1)
                if is_round(s + 2):
                    transpose_positions(s + 2)
                if is_round(s + 1):
                    quantise_by_position(s + 1)
                if is_round(s):
                    sum_w(s)
                    quantise_w(s)
                    second_matmul(s)
                if is_round(s + 1):
                    invert_totals(s + 1)
                if is_round(s + 2):
                    regroup_by_position(s + 2)
                if is_round(s + 3):
                    regroup_on_scalar(s + 3)
                if is_round(s + 1):
                    inverses_to_psum(s + 1)
